import numpy as np
import ml_dtypes


def mxq(x, axis, fmt="e4m3"):
    dtype, down = {"e4m3": (ml_dtypes.float8_e4m3fn, 7), "e5m2": (ml_dtypes.float8_e5m2, 14)}[fmt]
    v = np.moveaxis(np.asarray(x, np.float32).astype(ml_dtypes.bfloat16).astype(np.float64), axis, -1)
    blocks = v.reshape(v.shape[:-1] + (-1, 32))
    amax = np.abs(blocks).max(-1, keepdims=True)
    byte = np.maximum(np.where(amax > 0, np.frexp(amax)[1] - 1 + 127, 0) - down, 1)
    scale = np.exp2(byte - 127.0)
    codes = (blocks / scale).astype(np.float32).astype(dtype).astype(np.float64)
    return np.moveaxis((codes * scale).reshape(v.shape), -1, axis)


WIDE = False


def mx_kscale(k):
    if not WIDE:
        return np.ones(k)
    levels = np.array([20, -20, 10, -10, 0])
    a = np.random.permutation(np.resize(levels, k // 512 * 4)).reshape(k // 512, 4)
    idx = np.arange(k)
    return np.exp2(a[idx // 512, idx % 128 // 32])


BF16 = ml_dtypes.bfloat16


def bf(x):
    return np.asarray(x, np.float32).astype(BF16)


def f64(x):
    return np.asarray(x).astype(np.float64)


B, IN, OUT, N = 4096, 128, 512, 16
K = IN * N
MXB = 32
GS = 0.5


def chebyshev_basis(x, n):
    Ts = [np.ones_like(x), x]
    for _ in range(n - 2):
        Ts.append(2.0 * x * Ts[-1] - Ts[-2])
    return np.stack(Ts[:n], axis=-1)


def setup_inputs():
    wm = 2.0 / np.sqrt(K)
    x = np.random.uniform(-1.0, 1.0, (B, IN))
    w = np.random.uniform(-wm, wm, (OUT, IN, N))
    g = np.random.standard_normal((B, OUT)) * np.exp2(np.random.randint(-12, 1, (B, 1))) * GS
    sb = np.repeat(mx_kscale(B)[::MXB], MXB)
    t = (sb / sb.min())[:, None]
    y = (np.log(2.0 * t) + np.abs(x)) / (N - 1)
    x = np.where(t > 1.0, np.sign(x) * np.cosh(y), x)
    return {"x": bf(x), "w": bf(w), "grad_out": bf(g / t)}


def reference(x, w, grad_out):
    x, g = f64(x), f64(grad_out)
    n = w.shape[-1]
    basis = chebyshev_basis(x, n)
    bq = mxq(basis.reshape(x.shape[0], -1), 0, "e4m3")
    gq = mxq(g, 0, "e5m2")
    return (gq.T @ bq).reshape(g.shape[1], x.shape[1], n)

@@ -1,0 +1,223 @@
+from contextlib import ExitStack
+
+import concourse.mybir as mybir
+
+F32 = mybir.dt.float32
+BF16 = mybir.dt.bfloat16
+U32 = mybir.dt.uint32
+U8 = mybir.dt.uint8
+E4M3_X4 = mybir.dt.float8_e4m3fn_x4
+E5M2_X4 = mybir.dt.float8_e5m2_x4
+ACT = mybir.ActivationFunctionType
+ALU = mybir.AluOpType
+
+TOKENS, FEATURES, OUTPUTS, DEGREES = 4096, 128, 512, 16
+P = 128
+PACK = 4
+K_PASS = P * PACK
+PASSES = TOKENS // K_PASS
+N_TILE = 512
+M_TILE = 128
+O_TILES = OUTPUTS // M_TILE
+GROUP = N_TILE // DEGREES
+GROUPS = FEATURES // GROUP
+SLOT = GROUP * PACK
+TOKEN_PARTS = 2
+CHUNK_PASSES = PASSES // TOKEN_PARTS
+CHUNKS = GROUPS * TOKEN_PARTS
+
+FLOPS = 2 * TOKENS * OUTPUTS * FEATURES * DEGREES
+BYTES = 2 * TOKENS * FEATURES + 2 * TOKENS * OUTPUTS + 4 * OUTPUTS * FEATURES * DEGREES
+
+
+def tile_function_kernel(tc, x, w, grad_out, out):
+    nc = tc.nc
+    with ExitStack() as ctx:
+        keep = ctx.enter_context(tc.tile_pool(name="keep", bufs=1))
+        g_in = ctx.enter_context(tc.tile_pool(name="g_in", bufs=PASSES))
+        g_mid = ctx.enter_context(tc.tile_pool(name="g_mid", bufs=3))
+        work = ctx.enter_context(tc.tile_pool(name="work", bufs=2))
+        coded = ctx.enter_context(tc.tile_pool(name="coded", bufs=3))
+        result = ctx.enter_context(tc.tile_pool(name="result", bufs=4))
+        psum = ctx.enter_context(tc.psum_pool(name="psum", bufs=2))
+        ctx.enter_context(tc.manual_schedule())
+
+        x_rows = x.rearrange("(c p j) i -> p c j i", p=P, j=PACK)
+        x_raw = keep.tile([P, PASSES, PACK, FEATURES], BF16, name="x_raw")
+        g_rows = grad_out.rearrange("(c p j) o -> c p j o", p=P, j=PACK)
+        g_raw = []
+        for part in range(TOKEN_PARTS):
+            passes = slice(part * CHUNK_PASSES, (part + 1) * CHUNK_PASSES)
+            nc.sync.dma_start(out=x_raw[:, passes], in_=x_rows[:, passes])
+        for c in range(PASSES):
+            g_raw.append(g_in.tile([P, PACK, OUTPUTS], BF16, name="g_raw"))
+            nc.sync.dma_start(out=g_raw[c][:], in_=g_rows[c])
+
+        minus = {}
+        for value in (1.0, 2.0, 2.5):
+            minus[value] = keep.tile([P, 1], F32, name="minus_%d" % int(10 * value))
+            nc.vector.memset(minus[value][:], -value)
+        stages = []
+        for s in range(2):
+            stages.append(
+                keep.tile([P, CHUNK_PASSES, DEGREES, SLOT], BF16, name="stage%d" % s, align_bytes=64)
+            )
+            nc.vector.memset(stages[s][:, :, 0, :], 1.0)
+
+        g_codes = keep.tile([P, PASSES, OUTPUTS], U32, name="g_codes", align_bytes=64)
+        g_scales = keep.tile([P, PASSES, OUTPUTS], U8, name="g_scales", align_bytes=64)
+
+        def chunk_place(k):
+            return k // TOKEN_PARTS, k % TOKEN_PARTS
+
+        def quantise_grad_out(part):
+            grouped = {}
+            for c in range(part * CHUNK_PASSES, (part + 1) * CHUNK_PASSES):
+                grouped[c] = g_mid.tile([P, OUTPUTS, PACK], BF16, name="g_grouped", align_bytes=64)
+                dst = grouped[c][:].rearrange("p (a b) j -> p a j b", b=4)
+                src = g_raw[c][:].rearrange("p j (a b) -> p a j b", b=4)
+                if c % 2 == 0:
+                    nc.scalar.copy(out=dst, in_=src)
+                else:
+                    nc.vector.tensor_copy(out=dst, in_=src)
+                if c % 2 == 1:
+                    for done in (c - 1, c):
+                        nc.vector.quantize_mx(
+                            out=g_codes[:, done, :].bitcast(E5M2_X4),
+                            scales=g_scales[:, done, :],
+                            in_=grouped[done][:].rearrange("p o j -> p (o j)"),
+                        )
+
+        def degree_one(k):
+            group, part = chunk_place(k)
+            passes = slice(part * CHUNK_PASSES, (part + 1) * CHUNK_PASSES)
+            features = slice(group * GROUP, (group + 1) * GROUP)
+            nc.vector.tensor_copy(
+                out=stages[k % 2][:, :, 1, :].rearrange("p c (i j) -> p c i j", j=PACK),
+                in_=x_raw[:, passes, :, features].rearrange("p c j i -> p c i j"),
+            )
+
+        def basis(k):
+            stage = stages[k % 2]
+            t1 = stage[:, :, 1, :]
+
+            def f32_tile(name):
+                return work.tile([P, CHUNK_PASSES, SLOT], F32, name=name)
+
+            def square(name, src, scale, shift):
+                dst = f32_tile(name)
+                if shift == 0.0:
+                    nc.scalar.activation(out=dst[:], in_=src, func=ACT.Square, scale=scale)
+                else:
+                    nc.scalar.activation(
+                        out=dst[:], in_=src, func=ACT.Square, scale=scale, bias=minus[shift][:]
+                    )
+                return dst
+
+            def round_even(n, q_half):
+                nc.scalar.activation(
+                    out=stage[:, :, n, :], in_=q_half[:], func=ACT.Identity, scale=0.5,
+                    bias=minus[1.0][:],
+                )
+
+            def shifted_product(dst, a, shift, b):
+                nc.vector.scalar_tensor_tensor(
+                    out=dst, in0=a[:], scalar=shift, in1=b, op0=ALU.subtract, op1=ALU.mult
+                )
+
+            def minus_x(dst, a):
+                nc.vector.tensor_tensor(out=dst, in0=a[:], in1=t1, op=ALU.subtract)
+
+            def round_odd(n, t):
+                nc.vector.tensor_copy(out=stage[:, :, n, :], in_=t[:])
+
+            q1 = square("q1", t1, 2.0, 0.0)
+            q2 = square("q2", q1[:], 1.0, 2.0)
+            a5 = square("a5", q1[:], 1.0, 2.5)
+            q4 = square("q4", q2[:], 1.0, 2.0)
+            round_even(2, q1)
+            round_even(4, q2)
+            round_even(8, q4)
+
+            t3 = f32_tile("t3")
+            shifted_product(t3[:], q1, 3.0, t1)
+            t7 = f32_tile("t7")
+            shifted_product(t7[:], q2, 2.0, t3[:])
+            minus_x(t7[:], t7)
+            t5 = f32_tile("t5")
+            shifted_product(t5[:], a5, 1.25, t1)
+            round_odd(3, t3)
+            round_odd(5, t5)
+            round_odd(7, t7)
+
+            q3 = square("q3", t3[:], 2.0, 0.0)
+            q6 = square("q6", q3[:], 1.0, 2.0)
+            round_even(6, q3)
+            round_even(12, q6)
+            q5 = square("q5", t5[:], 2.0, 0.0)
+            round_even(10, q5)
+            q7 = square("q7", t7[:], 2.0, 0.0)
+            round_even(14, q7)
+
+            shifted_product(stage[:, :, 9, :], q3, 3.0, t3[:])
+            p11 = f32_tile("p11")
+            shifted_product(p11[:], q3, 2.0, t5[:])
+            minus_x(stage[:, :, 11, :], p11)
+            p13 = f32_tile("p13")
+            shifted_product(p13[:], q3, 2.0, t7[:])
+            minus_x(stage[:, :, 13, :], p13)
+            shifted_product(stage[:, :, 15, :], q5, 3.0, t5[:])
+
+        sums = {}
+
+        def quantise_and_multiply(k):
+            group, part = chunk_place(k)
+            stage = stages[k % 2]
+            b_codes = coded.tile([P, CHUNK_PASSES, N_TILE], U32, name="b_codes", align_bytes=64)
+            b_scales = coded.tile([P, CHUNK_PASSES, N_TILE], U8, name="b_scales", align_bytes=64)
+            if part == 0:
+                for t in range(O_TILES):
+                    sums[t] = psum.tile([M_TILE, N_TILE], F32, name="sums%d" % t)
+            for local in range(CHUNK_PASSES):
+                c = part * CHUNK_PASSES + local
+                nc.vector.quantize_mx(
+                    out=b_codes[:, local, :].bitcast(E4M3_X4),
+                    scales=b_scales[:, local, :],
+                    in_=stage[:, local, :, :].rearrange("p n e -> p (n e)"),
+                )
+                for t in range(O_TILES):
+                    o_cols = slice(t * M_TILE, (t + 1) * M_TILE)
+                    nc.tensor.matmul_mx(
+                        out=sums[t][:],
+                        lhsT=g_codes[:, c, o_cols].bitcast(E5M2_X4),
+                        lhsT_scale=g_scales[:, c, o_cols],
+                        rhs=b_codes[:, local, :].bitcast(E4M3_X4),
+                        rhs_scale=b_scales[:, local, :],
+                        start=(c == 0),
+                        stop=(c == PASSES - 1),
+                    )
+
+        out_rows = out.rearrange("o i n -> o (i n)")
+
+        def store_group(group):
+            for t in range(O_TILES):
+                ordered = result.tile([M_TILE, GROUP, DEGREES], F32, name="ordered")
+                nc.scalar.copy(out=ordered[:], in_=sums[t][:].rearrange("p (n i) -> p i n", n=DEGREES))
+                nc.sync.dma_start(
+                    out=out_rows[t * M_TILE : (t + 1) * M_TILE, group * N_TILE : (group + 1) * N_TILE],
+                    in_=ordered[:].rearrange("p i n -> p (i n)"),
+                )
+
+        degree_one(0)
+        for k in range(CHUNKS):
+            if k > 0:
+                quantise_and_multiply(k - 1)
+            basis(k)
+            if k + 1 < CHUNKS:
+                degree_one(k + 1)
+            if k < TOKEN_PARTS:
+                quantise_grad_out(k)
+            if k > 0 and k % TOKEN_PARTS == 0:
+                store_group(k // TOKEN_PARTS - 1)
+        quantise_and_multiply(CHUNKS - 1)
+        store_group(GROUPS - 1)

@@ -25,6 +25,7 @@ SLOT = GROUP * PACK
 TOKEN_PARTS = 2
 CHUNK_PASSES = PASSES // TOKEN_PARTS
 CHUNKS = GROUPS * TOKEN_PARTS
+STAGES = 3
 
 FLOPS = 2 * TOKENS * OUTPUTS * FEATURES * DEGREES
 BYTES = 2 * TOKENS * FEATURES + 2 * TOKENS * OUTPUTS + 4 * OUTPUTS * FEATURES * DEGREES
@@ -35,7 +36,7 @@ def tile_function_kernel(tc, x, w, grad_out, out):
     with ExitStack() as ctx:
         keep = ctx.enter_context(tc.tile_pool(name="keep", bufs=1))
         g_in = ctx.enter_context(tc.tile_pool(name="g_in", bufs=PASSES))
-        g_mid = ctx.enter_context(tc.tile_pool(name="g_mid", bufs=3))
+        g_mid = ctx.enter_context(tc.tile_pool(name="g_mid", bufs=CHUNK_PASSES))
         work = ctx.enter_context(tc.tile_pool(name="work", bufs=2))
         coded = ctx.enter_context(tc.tile_pool(name="coded", bufs=3))
         result = ctx.enter_context(tc.tile_pool(name="result", bufs=4))
@@ -58,7 +59,7 @@ def tile_function_kernel(tc, x, w, grad_out, out):
             minus[value] = keep.tile([P, 1], F32, name="minus_%d" % int(10 * value))
             nc.vector.memset(minus[value][:], -value)
         stages = []
-        for s in range(2):
+        for s in range(STAGES):
             stages.append(
                 keep.tile([P, CHUNK_PASSES, DEGREES, SLOT], BF16, name="stage%d" % s, align_bytes=64)
             )
@@ -66,129 +67,89 @@ def tile_function_kernel(tc, x, w, grad_out, out):
 
         g_codes = keep.tile([P, PASSES, OUTPUTS], U32, name="g_codes", align_bytes=64)
         g_scales = keep.tile([P, PASSES, OUTPUTS], U8, name="g_scales", align_bytes=64)
+        g_grouped = {}
 
-        def chunk_place(k):
-            return k // TOKEN_PARTS, k % TOKEN_PARTS
+        def slot(k, n):
+            return stages[k % STAGES][:, :, n, :]
 
-        def quantise_grad_out(part):
-            grouped = {}
+        def f32_tile(name):
+            return work.tile([P, CHUNK_PASSES, SLOT], F32, name=name)
+
+        def square(name, src, scale, shift):
+            dst = f32_tile(name)
+            if shift == 0.0:
+                nc.scalar.activation(out=dst[:], in_=src, func=ACT.Square, scale=scale)
+            else:
+                nc.scalar.activation(
+                    out=dst[:], in_=src, func=ACT.Square, scale=scale, bias=minus[shift][:]
+                )
+            return dst
+
+        def round_even(k, n, q_half):
+            nc.scalar.activation(
+                out=slot(k, n), in_=q_half[:], func=ACT.Identity, scale=0.5, bias=minus[1.0][:]
+            )
+
+        def shifted_product(dst, a, shift, b):
+            nc.vector.scalar_tensor_tensor(
+                out=dst, in0=a[:], scalar=shift, in1=b, op0=ALU.subtract, op1=ALU.mult
+            )
+
+        def minus_x(k, dst, a):
+            nc.vector.tensor_tensor(out=dst, in0=a[:], in1=slot(k, 1), op=ALU.subtract)
+
+        def round_odd(k, n, t):
+            nc.vector.tensor_copy(out=slot(k, n), in_=t[:])
+
+        def regroup_grad_out(part):
             for c in range(part * CHUNK_PASSES, (part + 1) * CHUNK_PASSES):
-                grouped[c] = g_mid.tile([P, OUTPUTS, PACK], BF16, name="g_grouped", align_bytes=64)
-                dst = grouped[c][:].rearrange("p (a b) j -> p a j b", b=4)
+                g_grouped[c] = g_mid.tile([P, OUTPUTS, PACK], BF16, name="g_grouped", align_bytes=64)
+                dst = g_grouped[c][:].rearrange("p (a b) j -> p a j b", b=4)
                 src = g_raw[c][:].rearrange("p j (a b) -> p a j b", b=4)
                 if c % 2 == 0:
                     nc.scalar.copy(out=dst, in_=src)
                 else:
                     nc.vector.tensor_copy(out=dst, in_=src)
-                if c % 2 == 1:
-                    for done in (c - 1, c):
-                        nc.vector.quantize_mx(
-                            out=g_codes[:, done, :].bitcast(E5M2_X4),
-                            scales=g_scales[:, done, :],
-                            in_=grouped[done][:].rearrange("p o j -> p (o j)"),
-                        )
+
+        def quantise_grad_out(part):
+            for c in range(part * CHUNK_PASSES, (part + 1) * CHUNK_PASSES):
+                nc.vector.quantize_mx(
+                    out=g_codes[:, c, :].bitcast(E5M2_X4),
+                    scales=g_scales[:, c, :],
+                    in_=g_grouped[c][:].rearrange("p o j -> p (o j)"),
+                )
 
         def degree_one(k):
-            group, part = chunk_place(k)
+            group, part = k // TOKEN_PARTS, k % TOKEN_PARTS
             passes = slice(part * CHUNK_PASSES, (part + 1) * CHUNK_PASSES)
             features = slice(group * GROUP, (group + 1) * GROUP)
             nc.vector.tensor_copy(
-                out=stages[k % 2][:, :, 1, :].rearrange("p c (i j) -> p c i j", j=PACK),
+                out=slot(k, 1).rearrange("p c (i j) -> p c i j", j=PACK),
                 in_=x_raw[:, passes, :, features].rearrange("p c j i -> p c i j"),
             )
-
-        def basis(k):
-            stage = stages[k % 2]
-            t1 = stage[:, :, 1, :]
-
-            def f32_tile(name):
-                return work.tile([P, CHUNK_PASSES, SLOT], F32, name=name)
-
-            def square(name, src, scale, shift):
-                dst = f32_tile(name)
-                if shift == 0.0:
-                    nc.scalar.activation(out=dst[:], in_=src, func=ACT.Square, scale=scale)
-                else:
-                    nc.scalar.activation(
-                        out=dst[:], in_=src, func=ACT.Square, scale=scale, bias=minus[shift][:]
-                    )
-                return dst
-
-            def round_even(n, q_half):
-                nc.scalar.activation(
-                    out=stage[:, :, n, :], in_=q_half[:], func=ACT.Identity, scale=0.5,
-                    bias=minus[1.0][:],
-                )
-
-            def shifted_product(dst, a, shift, b):
-                nc.vector.scalar_tensor_tensor(
-                    out=dst, in0=a[:], scalar=shift, in1=b, op0=ALU.subtract, op1=ALU.mult
-                )
-
-            def minus_x(dst, a):
-                nc.vector.tensor_tensor(out=dst, in0=a[:], in1=t1, op=ALU.subtract)
-
-            def round_odd(n, t):
-                nc.vector.tensor_copy(out=stage[:, :, n, :], in_=t[:])
-
-            q1 = square("q1", t1, 2.0, 0.0)
-            q2 = square("q2", q1[:], 1.0, 2.0)
-            a5 = square("a5", q1[:], 1.0, 2.5)
-            q4 = square("q4", q2[:], 1.0, 2.0)
-            round_even(2, q1)
-            round_even(4, q2)
-            round_even(8, q4)
-
-            t3 = f32_tile("t3")
-            shifted_product(t3[:], q1, 3.0, t1)
-            t7 = f32_tile("t7")
-            shifted_product(t7[:], q2, 2.0, t3[:])
-            minus_x(t7[:], t7)
-            t5 = f32_tile("t5")
-            shifted_product(t5[:], a5, 1.25, t1)
-            round_odd(3, t3)
-            round_odd(5, t5)
-            round_odd(7, t7)
-
-            q3 = square("q3", t3[:], 2.0, 0.0)
-            q6 = square("q6", q3[:], 1.0, 2.0)
-            round_even(6, q3)
-            round_even(12, q6)
-            q5 = square("q5", t5[:], 2.0, 0.0)
-            round_even(10, q5)
-            q7 = square("q7", t7[:], 2.0, 0.0)
-            round_even(14, q7)
-
-            shifted_product(stage[:, :, 9, :], q3, 3.0, t3[:])
-            p11 = f32_tile("p11")
-            shifted_product(p11[:], q3, 2.0, t5[:])
-            minus_x(stage[:, :, 11, :], p11)
-            p13 = f32_tile("p13")
-            shifted_product(p13[:], q3, 2.0, t7[:])
-            minus_x(stage[:, :, 13, :], p13)
-            shifted_product(stage[:, :, 15, :], q5, 3.0, t5[:])
 
         sums = {}
 
         def quantise_and_multiply(k):
-            group, part = chunk_place(k)
-            stage = stages[k % 2]
+            group, part = k // TOKEN_PARTS, k % TOKEN_PARTS
+            if group == 0:
+                quantise_grad_out(part)
             b_codes = coded.tile([P, CHUNK_PASSES, N_TILE], U32, name="b_codes", align_bytes=64)
             b_scales = coded.tile([P, CHUNK_PASSES, N_TILE], U8, name="b_scales", align_bytes=64)
             if part == 0:
                 for t in range(O_TILES):
-                    sums[t] = psum.tile([M_TILE, N_TILE], F32, name="sums%d" % t)
+                    sums[group, t] = psum.tile([M_TILE, N_TILE], F32, name="sums%d" % t)
             for local in range(CHUNK_PASSES):
                 c = part * CHUNK_PASSES + local
                 nc.vector.quantize_mx(
                     out=b_codes[:, local, :].bitcast(E4M3_X4),
                     scales=b_scales[:, local, :],
-                    in_=stage[:, local, :, :].rearrange("p n e -> p (n e)"),
+                    in_=stages[k % STAGES][:, local, :, :].rearrange("p n e -> p (n e)"),
                 )
                 for t in range(O_TILES):
                     o_cols = slice(t * M_TILE, (t + 1) * M_TILE)
                     nc.tensor.matmul_mx(
-                        out=sums[t][:],
+                        out=sums[group, t][:],
                         lhsT=g_codes[:, c, o_cols].bitcast(E5M2_X4),
                         lhsT_scale=g_scales[:, c, o_cols],
                         rhs=b_codes[:, local, :].bitcast(E4M3_X4),
@@ -202,22 +163,64 @@ def tile_function_kernel(tc, x, w, grad_out, out):
         def store_group(group):
             for t in range(O_TILES):
                 ordered = result.tile([M_TILE, GROUP, DEGREES], F32, name="ordered")
-                nc.scalar.copy(out=ordered[:], in_=sums[t][:].rearrange("p (n i) -> p i n", n=DEGREES))
+                by_feature = sums[group, t][:].rearrange("p (n i) -> p i n", n=DEGREES)
+                if group == GROUPS - 1 and t == O_TILES - 1:
+                    nc.vector.tensor_copy(out=ordered[:], in_=by_feature)
+                else:
+                    nc.scalar.copy(out=ordered[:], in_=by_feature)
                 nc.sync.dma_start(
                     out=out_rows[t * M_TILE : (t + 1) * M_TILE, group * N_TILE : (group + 1) * N_TILE],
                     in_=ordered[:].rearrange("p i n -> p (i n)"),
                 )
 
         degree_one(0)
+        q1 = square("q1", slot(0, 1), 2.0, 0.0)
+        q2 = square("q2", q1[:], 1.0, 2.0)
+        a5 = square("a5", q1[:], 1.0, 2.5)
         for k in range(CHUNKS):
+            more = k + 1 < CHUNKS
+            if more:
+                degree_one(k + 1)
+            t3 = f32_tile("t3")
+            shifted_product(t3[:], q1, 3.0, slot(k, 1))
+            t5 = f32_tile("t5")
+            shifted_product(t5[:], a5, 1.25, slot(k, 1))
+            t7 = f32_tile("t7")
+            shifted_product(t7[:], q2, 2.0, t3[:])
+            round_odd(k, 3, t3)
+            minus_x(k, t7[:], t7)
+            round_odd(k, 5, t5)
             if k > 0:
                 quantise_and_multiply(k - 1)
-            basis(k)
-            if k + 1 < CHUNKS:
-                degree_one(k + 1)
+            q4 = square("q4", q2[:], 1.0, 2.0)
+            round_even(k, 2, q1)
+            round_even(k, 4, q2)
+            round_even(k, 8, q4)
+            q3 = square("q3", t3[:], 2.0, 0.0)
+            q5 = square("q5", t5[:], 2.0, 0.0)
+            q6 = square("q6", q3[:], 1.0, 2.0)
+            round_even(k, 6, q3)
+            q7 = square("q7", t7[:], 2.0, 0.0)
+            round_even(k, 10, q5)
+            round_even(k, 12, q6)
+            if more:
+                q1 = square("q1", slot(k + 1, 1), 2.0, 0.0)
+            round_even(k, 14, q7)
+            if more:
+                q2 = square("q2", q1[:], 1.0, 2.0)
+                a5 = square("a5", q1[:], 1.0, 2.5)
+            p11 = f32_tile("p11")
+            shifted_product(p11[:], q3, 2.0, t5[:])
+            round_odd(k, 7, t7)
+            p13 = f32_tile("p13")
+            shifted_product(p13[:], q3, 2.0, t7[:])
+            shifted_product(slot(k, 9), q3, 3.0, t3[:])
+            minus_x(k, slot(k, 11), p11)
+            minus_x(k, slot(k, 13), p13)
+            shifted_product(slot(k, 15), q5, 3.0, t5[:])
             if k < TOKEN_PARTS:
-                quantise_grad_out(k)
-            if k > 0 and k % TOKEN_PARTS == 0:
+                regroup_grad_out(k)
+            if k > TOKEN_PARTS and k % TOKEN_PARTS == 1:
                 store_group(k // TOKEN_PARTS - 1)
         quantise_and_multiply(CHUNKS - 1)
         store_group(GROUPS - 1)

@@ -1,6 +1,7 @@
 from contextlib import ExitStack
 
 import concourse.mybir as mybir
+from concourse.masks import make_identity
 
 F32 = mybir.dt.float32
 BF16 = mybir.dt.bfloat16
@@ -31,16 +32,20 @@ FLOPS = 2 * TOKENS * OUTPUTS * FEATURES * DEGREES
 BYTES = 2 * TOKENS * FEATURES + 2 * TOKENS * OUTPUTS + 4 * OUTPUTS * FEATURES * DEGREES
 
 
+PE_REGROUP = False
+X_BANKS = 3
+
+
 def tile_function_kernel(tc, x, w, grad_out, out):
     nc = tc.nc
     with ExitStack() as ctx:
         keep = ctx.enter_context(tc.tile_pool(name="keep", bufs=1))
         g_in = ctx.enter_context(tc.tile_pool(name="g_in", bufs=PASSES))
-        g_mid = ctx.enter_context(tc.tile_pool(name="g_mid", bufs=CHUNK_PASSES))
+        g_mid = ctx.enter_context(tc.tile_pool(name="g_mid", bufs=PASSES if PE_REGROUP else CHUNK_PASSES))
         work = ctx.enter_context(tc.tile_pool(name="work", bufs=2))
         coded = ctx.enter_context(tc.tile_pool(name="coded", bufs=3))
         result = ctx.enter_context(tc.tile_pool(name="result", bufs=4))
-        psum = ctx.enter_context(tc.psum_pool(name="psum", bufs=2))
+        psum = ctx.enter_context(tc.psum_pool(name="psum", bufs=1))
         ctx.enter_context(tc.manual_schedule())
 
         x_rows = x.rearrange("(c p j) i -> p c j i", p=P, j=PACK)
@@ -54,6 +59,8 @@ def tile_function_kernel(tc, x, w, grad_out, out):
             g_raw.append(g_in.tile([P, PACK, OUTPUTS], BF16, name="g_raw"))
             nc.sync.dma_start(out=g_raw[c][:], in_=g_rows[c])
 
+        ident = keep.tile([P, P], BF16, name="ident")
+        make_identity(nc, ident[:])
         minus = {}
         for value in (1.0, 2.0, 2.5):
             minus[value] = keep.tile([P, 1], F32, name="minus_%d" % int(10 * value))
@@ -68,6 +75,7 @@ def tile_function_kernel(tc, x, w, grad_out, out):
         g_codes = keep.tile([P, PASSES, OUTPUTS], U32, name="g_codes", align_bytes=64)
         g_scales = keep.tile([P, PASSES, OUTPUTS], U8, name="g_scales", align_bytes=64)
         g_grouped = {}
+        x_psum = {}
 
         def slot(k, n):
             return stages[k % STAGES][:, :, n, :]
@@ -75,41 +83,48 @@ def tile_function_kernel(tc, x, w, grad_out, out):
         def f32_tile(name):
             return work.tile([P, CHUNK_PASSES, SLOT], F32, name=name)
 
-        def square(name, src, scale, shift):
-            dst = f32_tile(name)
+        def square(dst, src, scale, shift):
             if shift == 0.0:
-                nc.scalar.activation(out=dst[:], in_=src, func=ACT.Square, scale=scale)
+                nc.scalar.activation(out=dst, in_=src, func=ACT.Square, scale=scale)
             else:
-                nc.scalar.activation(
-                    out=dst[:], in_=src, func=ACT.Square, scale=scale, bias=minus[shift][:]
-                )
-            return dst
+                nc.scalar.activation(out=dst, in_=src, func=ACT.Square, scale=scale, bias=minus[shift][:])
 
         def round_even(k, n, q_half):
-            nc.scalar.activation(
-                out=slot(k, n), in_=q_half[:], func=ACT.Identity, scale=0.5, bias=minus[1.0][:]
-            )
+            nc.scalar.activation(out=slot(k, n), in_=q_half, func=ACT.Identity, scale=0.5, bias=minus[1.0][:])
 
         def shifted_product(dst, a, shift, b):
-            nc.vector.scalar_tensor_tensor(
-                out=dst, in0=a[:], scalar=shift, in1=b, op0=ALU.subtract, op1=ALU.mult
-            )
+            nc.vector.scalar_tensor_tensor(out=dst, in0=a, scalar=shift, in1=b, op0=ALU.subtract, op1=ALU.mult)
 
         def minus_x(k, dst, a):
-            nc.vector.tensor_tensor(out=dst, in0=a[:], in1=slot(k, 1), op=ALU.subtract)
-
-        def round_odd(k, n, t):
-            nc.vector.tensor_copy(out=slot(k, n), in_=t[:])
+            nc.vector.tensor_tensor(out=dst, in0=a, in1=x_psum[k][:], op=ALU.subtract)
 
         def regroup_grad_out(part):
             for c in range(part * CHUNK_PASSES, (part + 1) * CHUNK_PASSES):
                 g_grouped[c] = g_mid.tile([P, OUTPUTS, PACK], BF16, name="g_grouped", align_bytes=64)
-                dst = g_grouped[c][:].rearrange("p (a b) j -> p a j b", b=4)
-                src = g_raw[c][:].rearrange("p j (a b) -> p a j b", b=4)
-                if c % 2 == 0:
-                    nc.scalar.copy(out=dst, in_=src)
+                if PE_REGROUP:
+                    for half in range(2):
+                        bank = psum.tile([P, 2 * M_TILE, PACK], BF16, name="sums%d" % ((2 * c + half) % O_TILES))
+                        for q in range(2):
+                            o0 = (2 * half + q) * M_TILE
+                            nc.tensor.matmul(
+                                out=bank[:, q * M_TILE : (q + 1) * M_TILE, :],
+                                lhsT=ident[:],
+                                rhs=g_raw[c][:, :, o0 : o0 + M_TILE].rearrange("p j o -> p o j"),
+                                start=True,
+                                stop=True,
+                            )
+                        dst = g_grouped[c][:, 2 * half * M_TILE : 2 * (half + 1) * M_TILE, :]
+                        if c % 2 == 0:
+                            nc.scalar.copy(out=dst, in_=bank[:])
+                        else:
+                            nc.vector.tensor_copy(out=dst, in_=bank[:])
                 else:
-                    nc.vector.tensor_copy(out=dst, in_=src)
+                    dst = g_grouped[c][:].rearrange("p (a b) j -> p a j b", b=4)
+                    src = g_raw[c][:].rearrange("p j (a b) -> p a j b", b=4)
+                    if c % 2 == 0:
+                        nc.scalar.copy(out=dst, in_=src)
+                    else:
+                        nc.vector.tensor_copy(out=dst, in_=src)
 
         def quantise_grad_out(part):
             for c in range(part * CHUNK_PASSES, (part + 1) * CHUNK_PASSES):
@@ -127,10 +142,12 @@ def tile_function_kernel(tc, x, w, grad_out, out):
                 out=slot(k, 1).rearrange("p c (i j) -> p c i j", j=PACK),
                 in_=x_raw[:, passes, :, features].rearrange("p c j i -> p c i j"),
             )
+            x_psum[k] = psum.tile([P, CHUNK_PASSES, SLOT], F32, name="xp", bufs=X_BANKS)
+            nc.tensor.matmul(out=x_psum[k][:], lhsT=ident[:], rhs=slot(k, 1), start=True, stop=True)
 
         sums = {}
 
-        def quantise_and_multiply(k):
+        def quantise_and_multiply(k, after_first):
             group, part = k // TOKEN_PARTS, k % TOKEN_PARTS
             if group == 0:
                 quantise_grad_out(part)
@@ -157,6 +174,8 @@ def tile_function_kernel(tc, x, w, grad_out, out):
                         start=(c == 0),
                         stop=(c == PASSES - 1),
                     )
+                if local == 0:
+                    after_first()
 
         out_rows = out.rearrange("o i n -> o (i n)")
 
@@ -173,54 +192,92 @@ def tile_function_kernel(tc, x, w, grad_out, out):
                     in_=ordered[:].rearrange("p i n -> p (i n)"),
                 )
 
+        late = {}
+
+        def finish_chunk(k):
+            p11, p13, odd_squares = late[k]
+            shot = work.tile([P, 1], F32, name="shot")
+            nc.vector.memset(shot[:], 0.5)
+            nc.gpsimd.tensor_scalar(
+                out=stages[k % STAGES][:, :, 6:15:4, :],
+                in0=odd_squares[:].rearrange("p q c e -> p c q e"),
+                scalar1=shot[:, 0:1],
+                scalar2=-1.0,
+                op0=ALU.mult,
+                op1=ALU.add,
+            )
+            minus_x(k, slot(k, 11), p11[:])
+            minus_x(k, slot(k, 13), p13[:])
+
+        def nothing():
+            return None
+
         degree_one(0)
-        q1 = square("q1", slot(0, 1), 2.0, 0.0)
-        q2 = square("q2", q1[:], 1.0, 2.0)
-        a5 = square("a5", q1[:], 1.0, 2.5)
+        q1 = f32_tile("q1")
+        square(q1[:], slot(0, 1), 2.0, 0.0)
+        q2 = f32_tile("q2")
+        square(q2[:], q1[:], 1.0, 2.0)
+        a5 = f32_tile("a5")
+        square(a5[:], q1[:], 1.0, 2.5)
         for k in range(CHUNKS):
             more = k + 1 < CHUNKS
             if more:
                 degree_one(k + 1)
-            t3 = f32_tile("t3")
-            shifted_product(t3[:], q1, 3.0, slot(k, 1))
-            t5 = f32_tile("t5")
-            shifted_product(t5[:], a5, 1.25, slot(k, 1))
-            t7 = f32_tile("t7")
-            shifted_product(t7[:], q2, 2.0, t3[:])
-            round_odd(k, 3, t3)
-            minus_x(k, t7[:], t7)
-            round_odd(k, 5, t5)
             if k > 0:
-                quantise_and_multiply(k - 1)
-            q4 = square("q4", q2[:], 1.0, 2.0)
-            round_even(k, 2, q1)
-            round_even(k, 4, q2)
-            round_even(k, 8, q4)
-            q3 = square("q3", t3[:], 2.0, 0.0)
-            q5 = square("q5", t5[:], 2.0, 0.0)
-            q6 = square("q6", q3[:], 1.0, 2.0)
-            round_even(k, 6, q3)
-            q7 = square("q7", t7[:], 2.0, 0.0)
-            round_even(k, 10, q5)
-            round_even(k, 12, q6)
+                finish_chunk(k - 1)
+            t3 = f32_tile("t3")
+            shifted_product(t3[:], q1[:], 3.0, x_psum[k][:])
+            t5 = f32_tile("t5")
+            shifted_product(t5[:], a5[:], 1.25, x_psum[k][:])
+            t7 = f32_tile("t7")
+            shifted_product(t7[:], q2[:], 2.0, t3[:])
+
+            def seventh(k=k, t7=t7):
+                minus_x(k, t7[:], t7[:])
+
+            if PE_REGROUP and k == 1:
+                regroup_grad_out(1)
+            if k > 0:
+                quantise_and_multiply(k - 1, seventh)
+            else:
+                seventh()
+            odd_squares = work.tile([P, 3, CHUNK_PASSES, SLOT], F32, name="odd_squares")
+            q3, q5, q7 = odd_squares[:, 0], odd_squares[:, 1], odd_squares[:, 2]
+            q4 = f32_tile("q4")
+            square(q4[:], q2[:], 1.0, 2.0)
+            round_even(k, 2, q1[:])
+            round_even(k, 4, q2[:])
+            round_even(k, 8, q4[:])
+            square(q3, t3[:], 2.0, 0.0)
+            square(q5, t5[:], 2.0, 0.0)
+            nc.scalar.copy(out=slot(k, 3), in_=t3[:])
+            q6 = f32_tile("q6")
+            square(q6[:], q3, 1.0, 2.0)
+            nc.scalar.copy(out=slot(k, 5), in_=t5[:])
+            round_even(k, 12, q6[:])
+            square(q7, t7[:], 2.0, 0.0)
             if more:
-                q1 = square("q1", slot(k + 1, 1), 2.0, 0.0)
-            round_even(k, 14, q7)
-            if more:
-                q2 = square("q2", q1[:], 1.0, 2.0)
-                a5 = square("a5", q1[:], 1.0, 2.5)
+                q1 = f32_tile("q1")
+                square(q1[:], slot(k + 1, 1), 2.0, 0.0)
+                q2 = f32_tile("q2")
+                square(q2[:], q1[:], 1.0, 2.0)
+                a5 = f32_tile("a5")
+                square(a5[:], q1[:], 1.0, 2.5)
+            nc.vector.tensor_copy(out=slot(k, 7), in_=t7[:])
             p11 = f32_tile("p11")
             shifted_product(p11[:], q3, 2.0, t5[:])
-            round_odd(k, 7, t7)
             p13 = f32_tile("p13")
             shifted_product(p13[:], q3, 2.0, t7[:])
             shifted_product(slot(k, 9), q3, 3.0, t3[:])
-            minus_x(k, slot(k, 11), p11)
-            minus_x(k, slot(k, 13), p13)
             shifted_product(slot(k, 15), q5, 3.0, t5[:])
-            if k < TOKEN_PARTS:
+            late[k] = (p11, p13, odd_squares)
+            if PE_REGROUP:
+                if k == 0:
+                    regroup_grad_out(0)
+            elif k < TOKEN_PARTS:
                 regroup_grad_out(k)
-            if k > TOKEN_PARTS and k % TOKEN_PARTS == 1:
+            if k >= TOKEN_PARTS and k % TOKEN_PARTS == 0:
                 store_group(k // TOKEN_PARTS - 1)
-        quantise_and_multiply(CHUNKS - 1)
+        finish_chunk(CHUNKS - 1)
+        quantise_and_multiply(CHUNKS - 1, nothing)
         store_group(GROUPS - 1)

@@ -32,16 +32,25 @@ FLOPS = 2 * TOKENS * OUTPUTS * FEATURES * DEGREES
 BYTES = 2 * TOKENS * FEATURES + 2 * TOKENS * OUTPUTS + 4 * OUTPUTS * FEATURES * DEGREES
 
 
-PE_REGROUP = False
 X_BANKS = 3
+SIZES = (4, 4)
+LAST_SIZES = (4, 2, 2)
+SCALAR_TAIL = 1
 
 
 def tile_function_kernel(tc, x, w, grad_out, out):
     nc = tc.nc
+    chunks = []
+    for group in range(GROUPS):
+        first = 0
+        for size in LAST_SIZES if group == GROUPS - 1 else SIZES:
+            chunks.append((group, first, size))
+            first += size
+    count = len(chunks)
     with ExitStack() as ctx:
         keep = ctx.enter_context(tc.tile_pool(name="keep", bufs=1))
         g_in = ctx.enter_context(tc.tile_pool(name="g_in", bufs=PASSES))
-        g_mid = ctx.enter_context(tc.tile_pool(name="g_mid", bufs=PASSES if PE_REGROUP else CHUNK_PASSES))
+        g_mid = ctx.enter_context(tc.tile_pool(name="g_mid", bufs=CHUNK_PASSES))
         work = ctx.enter_context(tc.tile_pool(name="work", bufs=2))
         coded = ctx.enter_context(tc.tile_pool(name="coded", bufs=3))
         result = ctx.enter_context(tc.tile_pool(name="result", bufs=4))
@@ -61,6 +70,8 @@ def tile_function_kernel(tc, x, w, grad_out, out):
 
         ident = keep.tile([P, P], BF16, name="ident")
         make_identity(nc, ident[:])
+        ident32 = keep.tile([P, P], F32, name="ident32")
+        make_identity(nc, ident32[:])
         minus = {}
         for value in (1.0, 2.0, 2.5):
             minus[value] = keep.tile([P, 1], F32, name="minus_%d" % int(10 * value))
@@ -77,11 +88,19 @@ def tile_function_kernel(tc, x, w, grad_out, out):
         g_grouped = {}
         x_psum = {}
 
-        def slot(k, n):
-            return stages[k % STAGES][:, :, n, :]
+        def size_of(k):
+            return chunks[k][2]
 
-        def f32_tile(name):
-            return work.tile([P, CHUNK_PASSES, SLOT], F32, name=name)
+        def slot(k, n):
+            return stages[k % STAGES][:, : size_of(k), n, :]
+
+        def f32_tile(k, name):
+            whole = work.tile([P, CHUNK_PASSES, SLOT], F32, name=name)
+            return whole[:, : size_of(k), :]
+
+        def f32_tiles(k, name, how_many):
+            whole = work.tile([P, how_many, CHUNK_PASSES, SLOT], F32, name=name)
+            return whole[:, :, : size_of(k), :]
 
         def square(dst, src, scale, shift):
             if shift == 0.0:
@@ -96,68 +115,61 @@ def tile_function_kernel(tc, x, w, grad_out, out):
             nc.vector.scalar_tensor_tensor(out=dst, in0=a, scalar=shift, in1=b, op0=ALU.subtract, op1=ALU.mult)
 
         def minus_x(k, dst, a):
-            nc.vector.tensor_tensor(out=dst, in0=a, in1=x_psum[k][:], op=ALU.subtract)
+            nc.vector.tensor_tensor(out=dst, in0=a, in1=x_psum[k], op=ALU.subtract)
+
+        def evens_on_gpsimd(k, squares, degrees):
+            shot = work.tile([P, 1], F32, name="shot", bufs=4)
+            nc.vector.memset(shot[:], 0.5)
+            nc.gpsimd.tensor_scalar(
+                out=stages[k % STAGES][:, : size_of(k), degrees, :],
+                in0=squares.rearrange("p q c e -> p c q e"),
+                scalar1=shot[:, 0:1],
+                scalar2=-1.0,
+                op0=ALU.mult,
+                op1=ALU.add,
+            )
 
         def regroup_grad_out(part):
             for c in range(part * CHUNK_PASSES, (part + 1) * CHUNK_PASSES):
                 g_grouped[c] = g_mid.tile([P, OUTPUTS, PACK], BF16, name="g_grouped", align_bytes=64)
-                if PE_REGROUP:
-                    for half in range(2):
-                        bank = psum.tile([P, 2 * M_TILE, PACK], BF16, name="sums%d" % ((2 * c + half) % O_TILES))
-                        for q in range(2):
-                            o0 = (2 * half + q) * M_TILE
-                            nc.tensor.matmul(
-                                out=bank[:, q * M_TILE : (q + 1) * M_TILE, :],
-                                lhsT=ident[:],
-                                rhs=g_raw[c][:, :, o0 : o0 + M_TILE].rearrange("p j o -> p o j"),
-                                start=True,
-                                stop=True,
-                            )
-                        dst = g_grouped[c][:, 2 * half * M_TILE : 2 * (half + 1) * M_TILE, :]
-                        if c % 2 == 0:
-                            nc.scalar.copy(out=dst, in_=bank[:])
-                        else:
-                            nc.vector.tensor_copy(out=dst, in_=bank[:])
+                dst = g_grouped[c][:].rearrange("p (a b) j -> p a j b", b=4)
+                src = g_raw[c][:].rearrange("p j (a b) -> p a j b", b=4)
+                if c % 2 == 0:
+                    nc.scalar.copy(out=dst, in_=src)
                 else:
-                    dst = g_grouped[c][:].rearrange("p (a b) j -> p a j b", b=4)
-                    src = g_raw[c][:].rearrange("p j (a b) -> p a j b", b=4)
-                    if c % 2 == 0:
-                        nc.scalar.copy(out=dst, in_=src)
-                    else:
-                        nc.vector.tensor_copy(out=dst, in_=src)
-
-        def quantise_grad_out(part):
-            for c in range(part * CHUNK_PASSES, (part + 1) * CHUNK_PASSES):
-                nc.vector.quantize_mx(
-                    out=g_codes[:, c, :].bitcast(E5M2_X4),
-                    scales=g_scales[:, c, :],
-                    in_=g_grouped[c][:].rearrange("p o j -> p (o j)"),
-                )
+                    nc.vector.tensor_copy(out=dst, in_=src)
 
         def degree_one(k):
-            group, part = k // TOKEN_PARTS, k % TOKEN_PARTS
-            passes = slice(part * CHUNK_PASSES, (part + 1) * CHUNK_PASSES)
+            group, first, size = chunks[k]
             features = slice(group * GROUP, (group + 1) * GROUP)
-            nc.vector.tensor_copy(
-                out=slot(k, 1).rearrange("p c (i j) -> p c i j", j=PACK),
-                in_=x_raw[:, passes, :, features].rearrange("p c j i -> p c i j"),
-            )
-            x_psum[k] = psum.tile([P, CHUNK_PASSES, SLOT], F32, name="xp", bufs=X_BANKS)
-            nc.tensor.matmul(out=x_psum[k][:], lhsT=ident[:], rhs=slot(k, 1), start=True, stop=True)
+            dst = slot(k, 1).rearrange("p c (i j) -> p c i j", j=PACK)
+            src = x_raw[:, first : first + size, :, features].rearrange("p c j i -> p c i j")
+            if False:
+                nc.scalar.copy(out=dst, in_=src)
+            else:
+                nc.vector.tensor_copy(out=dst, in_=src)
+            bank = psum.tile([P, CHUNK_PASSES, SLOT], F32, name="xp", bufs=X_BANKS)
+            x_psum[k] = bank[:, :size, :]
+            nc.tensor.matmul(out=x_psum[k], lhsT=ident[:], rhs=slot(k, 1), start=True, stop=True)
 
         sums = {}
 
         def quantise_and_multiply(k, after_first):
-            group, part = k // TOKEN_PARTS, k % TOKEN_PARTS
+            group, first, size = chunks[k]
             if group == 0:
-                quantise_grad_out(part)
+                for c in range(first, first + size):
+                    nc.vector.quantize_mx(
+                        out=g_codes[:, c, :].bitcast(E5M2_X4),
+                        scales=g_scales[:, c, :],
+                        in_=g_grouped[c][:].rearrange("p o j -> p (o j)"),
+                    )
             b_codes = coded.tile([P, CHUNK_PASSES, N_TILE], U32, name="b_codes", align_bytes=64)
             b_scales = coded.tile([P, CHUNK_PASSES, N_TILE], U8, name="b_scales", align_bytes=64)
-            if part == 0:
+            if first == 0:
                 for t in range(O_TILES):
                     sums[group, t] = psum.tile([M_TILE, N_TILE], F32, name="sums%d" % t)
-            for local in range(CHUNK_PASSES):
-                c = part * CHUNK_PASSES + local
+            for local in range(size):
+                c = first + local
                 nc.vector.quantize_mx(
                     out=b_codes[:, local, :].bitcast(E4M3_X4),
                     scales=b_scales[:, local, :],
@@ -183,7 +195,7 @@ def tile_function_kernel(tc, x, w, grad_out, out):
             for t in range(O_TILES):
                 ordered = result.tile([M_TILE, GROUP, DEGREES], F32, name="ordered")
                 by_feature = sums[group, t][:].rearrange("p (n i) -> p i n", n=DEGREES)
-                if group == GROUPS - 1 and t == O_TILES - 1:
+                if group == GROUPS - 1 and t % 2 == 1:
                     nc.vector.tensor_copy(out=ordered[:], in_=by_feature)
                 else:
                     nc.scalar.copy(out=ordered[:], in_=by_feature)
@@ -194,90 +206,98 @@ def tile_function_kernel(tc, x, w, grad_out, out):
 
         late = {}
 
+        def with_gpsimd(k):
+            return k < count - SCALAR_TAIL
+
         def finish_chunk(k):
             p11, p13, odd_squares = late[k]
-            shot = work.tile([P, 1], F32, name="shot")
-            nc.vector.memset(shot[:], 0.5)
-            nc.gpsimd.tensor_scalar(
-                out=stages[k % STAGES][:, :, 6:15:4, :],
-                in0=odd_squares[:].rearrange("p q c e -> p c q e"),
-                scalar1=shot[:, 0:1],
-                scalar2=-1.0,
-                op0=ALU.mult,
-                op1=ALU.add,
-            )
-            minus_x(k, slot(k, 11), p11[:])
-            minus_x(k, slot(k, 13), p13[:])
+            if with_gpsimd(k):
+                evens_on_gpsimd(k, odd_squares, slice(6, 15, 4))
+            minus_x(k, slot(k, 11), p11)
+            minus_x(k, slot(k, 13), p13)
 
         def nothing():
             return None
 
+        def first_squares(k):
+            q1 = f32_tile(k, "q1")
+            square(q1, slot(k, 1), 2.0, 0.0)
+            q2 = f32_tile(k, "q2")
+            square(q2, q1, 1.0, 2.0)
+            a5 = f32_tile(k, "a5")
+            square(a5, q1, 1.0, 2.5)
+            return q1, q2, a5
+
         degree_one(0)
-        q1 = f32_tile("q1")
-        square(q1[:], slot(0, 1), 2.0, 0.0)
-        q2 = f32_tile("q2")
-        square(q2[:], q1[:], 1.0, 2.0)
-        a5 = f32_tile("a5")
-        square(a5[:], q1[:], 1.0, 2.5)
-        for k in range(CHUNKS):
-            more = k + 1 < CHUNKS
+        q1, q2, a5 = first_squares(0)
+        for k in range(count):
+            more = k + 1 < count
             if more:
                 degree_one(k + 1)
             if k > 0:
                 finish_chunk(k - 1)
-            t3 = f32_tile("t3")
-            shifted_product(t3[:], q1[:], 3.0, x_psum[k][:])
-            t5 = f32_tile("t5")
-            shifted_product(t5[:], a5[:], 1.25, x_psum[k][:])
-            t7 = f32_tile("t7")
-            shifted_product(t7[:], q2[:], 2.0, t3[:])
+            t3 = f32_tile(k, "t3")
+            shifted_product(t3, q1, 3.0, x_psum[k])
+            t5 = f32_tile(k, "t5")
+            shifted_product(t5, a5, 1.25, x_psum[k])
+            t7 = f32_tile(k, "t7")
+            shifted_product(t7, q2, 2.0, t3)
+            odd_squares = f32_tiles(k, "odd_squares", 3)
+            q3, q5, q7 = odd_squares[:, 0], odd_squares[:, 1], odd_squares[:, 2]
+            even_squares = f32_tiles(k, "even_squares", 2)
+            q4, q6 = even_squares[:, 0], even_squares[:, 1]
+            if True:
+                square(q3, t3, 2.0, 0.0)
+            square(q4, q2, 1.0, 2.0)
+            round_even(k, 2, q1)
+            round_even(k, 4, q2)
+            if not (True):
+                square(q3, t3, 2.0, 0.0)
+            if with_gpsimd(k):
+                bank = psum.tile([P, CHUNK_PASSES, SLOT], F32, name="q3p")
+                q3_psum = bank[:, : size_of(k), :]
+                nc.tensor.matmul(out=q3_psum, lhsT=ident32[:], rhs=q3, start=True, stop=True)
+            else:
+                q3_psum = q3
 
             def seventh(k=k, t7=t7):
-                minus_x(k, t7[:], t7[:])
+                minus_x(k, t7, t7)
 
-            if PE_REGROUP and k == 1:
-                regroup_grad_out(1)
             if k > 0:
                 quantise_and_multiply(k - 1, seventh)
             else:
                 seventh()
-            odd_squares = work.tile([P, 3, CHUNK_PASSES, SLOT], F32, name="odd_squares")
-            q3, q5, q7 = odd_squares[:, 0], odd_squares[:, 1], odd_squares[:, 2]
-            q4 = f32_tile("q4")
-            square(q4[:], q2[:], 1.0, 2.0)
-            round_even(k, 2, q1[:])
-            round_even(k, 4, q2[:])
-            round_even(k, 8, q4[:])
-            square(q3, t3[:], 2.0, 0.0)
-            square(q5, t5[:], 2.0, 0.0)
-            nc.scalar.copy(out=slot(k, 3), in_=t3[:])
-            q6 = f32_tile("q6")
-            square(q6[:], q3, 1.0, 2.0)
-            nc.scalar.copy(out=slot(k, 5), in_=t5[:])
-            round_even(k, 12, q6[:])
-            square(q7, t7[:], 2.0, 0.0)
+            square(q5, t5, 2.0, 0.0)
+            nc.scalar.copy(out=slot(k, 3), in_=t3)
+            square(q6, q3, 1.0, 2.0)
+            nc.scalar.copy(out=slot(k, 5), in_=t5)
+            square(q7, t7, 2.0, 0.0)
+            if not with_gpsimd(k):
+                round_even(k, 8, q4)
+                round_even(k, 6, q3)
+                round_even(k, 10, q5)
+                round_even(k, 12, q6)
+            if True:
+                nc.scalar.copy(out=slot(k, 7), in_=t7)
+            if not with_gpsimd(k):
+                round_even(k, 14, q7)
             if more:
-                q1 = f32_tile("q1")
-                square(q1[:], slot(k + 1, 1), 2.0, 0.0)
-                q2 = f32_tile("q2")
-                square(q2[:], q1[:], 1.0, 2.0)
-                a5 = f32_tile("a5")
-                square(a5[:], q1[:], 1.0, 2.5)
-            nc.vector.tensor_copy(out=slot(k, 7), in_=t7[:])
-            p11 = f32_tile("p11")
-            shifted_product(p11[:], q3, 2.0, t5[:])
-            p13 = f32_tile("p13")
-            shifted_product(p13[:], q3, 2.0, t7[:])
-            shifted_product(slot(k, 9), q3, 3.0, t3[:])
-            shifted_product(slot(k, 15), q5, 3.0, t5[:])
+                q1, q2, a5 = first_squares(k + 1)
+            if not (True):
+                nc.vector.tensor_copy(out=slot(k, 7), in_=t7)
+            if with_gpsimd(k):
+                evens_on_gpsimd(k, even_squares, slice(8, 13, 4))
+            p11 = f32_tile(k, "p11")
+            shifted_product(p11, q3_psum, 2.0, t5)
+            p13 = f32_tile(k, "p13")
+            shifted_product(p13, q3_psum, 2.0, t7)
+            shifted_product(slot(k, 9), q3_psum, 3.0, t3)
+            shifted_product(slot(k, 15), q5, 3.0, t5)
             late[k] = (p11, p13, odd_squares)
-            if PE_REGROUP:
-                if k == 0:
-                    regroup_grad_out(0)
-            elif k < TOKEN_PARTS:
+            if k < TOKEN_PARTS:
                 regroup_grad_out(k)
-            if k >= TOKEN_PARTS and k % TOKEN_PARTS == 0:
-                store_group(k // TOKEN_PARTS - 1)
-        finish_chunk(CHUNKS - 1)
-        quantise_and_multiply(CHUNKS - 1, nothing)
+            if k > 0 and chunks[k - 1][1] + chunks[k - 1][2] == PASSES:
+                store_group(chunks[k - 1][0])
+        finish_chunk(count - 1)
+        quantise_and_multiply(count - 1, nothing)
         store_group(GROUPS - 1)

@@ -144,7 +144,7 @@ def tile_function_kernel(tc, x, w, grad_out, out):
             features = slice(group * GROUP, (group + 1) * GROUP)
             dst = slot(k, 1).rearrange("p c (i j) -> p c i j", j=PACK)
             src = x_raw[:, first : first + size, :, features].rearrange("p c j i -> p c i j")
-            if False:
+            if k > 1:
                 nc.scalar.copy(out=dst, in_=src)
             else:
                 nc.vector.tensor_copy(out=dst, in_=src)
@@ -154,7 +154,7 @@ def tile_function_kernel(tc, x, w, grad_out, out):
 
         sums = {}
 
-        def quantise_and_multiply(k, after_first):
+        def quantise_and_multiply(k):
             group, first, size = chunks[k]
             if group == 0:
                 for c in range(first, first + size):
@@ -186,8 +186,6 @@ def tile_function_kernel(tc, x, w, grad_out, out):
                         start=(c == 0),
                         stop=(c == PASSES - 1),
                     )
-                if local == 0:
-                    after_first()
 
         out_rows = out.rearrange("o i n -> o (i n)")
 
@@ -216,26 +214,28 @@ def tile_function_kernel(tc, x, w, grad_out, out):
             minus_x(k, slot(k, 11), p11)
             minus_x(k, slot(k, 13), p13)
 
+        def first_squares(k, between):
+            q1 = f32_tile(k, "q1")
+            square(q1, slot(k, 1), 2.0, 0.0)
+            between()
+            even_squares = f32_tiles(k, "even_squares", 3)
+            square(even_squares[:, 0], q1, 1.0, 2.0)
+            a5 = f32_tile(k, "a5")
+            square(a5, q1, 1.0, 2.5)
+            return q1, even_squares, a5
+
         def nothing():
             return None
 
-        def first_squares(k):
-            q1 = f32_tile(k, "q1")
-            square(q1, slot(k, 1), 2.0, 0.0)
-            q2 = f32_tile(k, "q2")
-            square(q2, q1, 1.0, 2.0)
-            a5 = f32_tile(k, "a5")
-            square(a5, q1, 1.0, 2.5)
-            return q1, q2, a5
-
         degree_one(0)
-        q1, q2, a5 = first_squares(0)
+        q1, even_squares, a5 = first_squares(0, nothing)
         for k in range(count):
             more = k + 1 < count
             if more:
                 degree_one(k + 1)
             if k > 0:
                 finish_chunk(k - 1)
+            q2, q4, q6 = even_squares[:, 0], even_squares[:, 1], even_squares[:, 2]
             t3 = f32_tile(k, "t3")
             shifted_product(t3, q1, 3.0, x_psum[k])
             t5 = f32_tile(k, "t5")
@@ -244,60 +244,61 @@ def tile_function_kernel(tc, x, w, grad_out, out):
             shifted_product(t7, q2, 2.0, t3)
             odd_squares = f32_tiles(k, "odd_squares", 3)
             q3, q5, q7 = odd_squares[:, 0], odd_squares[:, 1], odd_squares[:, 2]
-            even_squares = f32_tiles(k, "even_squares", 2)
-            q4, q6 = even_squares[:, 0], even_squares[:, 1]
-            if True:
-                square(q3, t3, 2.0, 0.0)
+            square(q3, t3, 2.0, 0.0)
             square(q4, q2, 1.0, 2.0)
-            round_even(k, 2, q1)
-            round_even(k, 4, q2)
-            if not (True):
-                square(q3, t3, 2.0, 0.0)
+            square(q6, q3, 1.0, 2.0)
             if with_gpsimd(k):
                 bank = psum.tile([P, CHUNK_PASSES, SLOT], F32, name="q3p")
                 q3_psum = bank[:, : size_of(k), :]
                 nc.tensor.matmul(out=q3_psum, lhsT=ident32[:], rhs=q3, start=True, stop=True)
             else:
                 q3_psum = q3
-
-            def seventh(k=k, t7=t7):
-                minus_x(k, t7, t7)
-
+            if k == 0:
+                nc.vector.tensor_copy(out=slot(k, 3), in_=t3)
             if k > 0:
-                quantise_and_multiply(k - 1, seventh)
-            else:
-                seventh()
+                quantise_and_multiply(k - 1)
+            if k == 0:
+                nc.vector.tensor_copy(out=slot(k, 5), in_=t5)
             square(q5, t5, 2.0, 0.0)
-            nc.scalar.copy(out=slot(k, 3), in_=t3)
-            square(q6, q3, 1.0, 2.0)
-            nc.scalar.copy(out=slot(k, 5), in_=t5)
-            square(q7, t7, 2.0, 0.0)
+            if not (k == 0):
+                nc.scalar.copy(out=slot(k, 3), in_=t3)
+            round_even(k, 2, q1)
+            if not (k == 0):
+                nc.scalar.copy(out=slot(k, 5), in_=t5)
+            if with_gpsimd(k):
+                evens_on_gpsimd(k, even_squares, slice(4, 13, 4))
+            minus_x(k, t7, t7)
             if not with_gpsimd(k):
+                round_even(k, 4, q2)
                 round_even(k, 8, q4)
                 round_even(k, 6, q3)
                 round_even(k, 10, q5)
                 round_even(k, 12, q6)
-            if True:
-                nc.scalar.copy(out=slot(k, 7), in_=t7)
+            old = (q3, q5, q7, t7, k)
+
+            def seventh(old=old):
+                square(old[2], old[3], 2.0, 0.0)
+
+            if more:
+                q1_next, even_next, a5_next = first_squares(k + 1, seventh)
+            else:
+                seventh()
+            nc.scalar.copy(out=slot(k, 7), in_=t7)
             if not with_gpsimd(k):
                 round_even(k, 14, q7)
-            if more:
-                q1, q2, a5 = first_squares(k + 1)
-            if not (True):
-                nc.vector.tensor_copy(out=slot(k, 7), in_=t7)
-            if with_gpsimd(k):
-                evens_on_gpsimd(k, even_squares, slice(8, 13, 4))
             p11 = f32_tile(k, "p11")
             shifted_product(p11, q3_psum, 2.0, t5)
+            shifted_product(slot(k, 9), q3_psum, 3.0, t3)
             p13 = f32_tile(k, "p13")
             shifted_product(p13, q3_psum, 2.0, t7)
-            shifted_product(slot(k, 9), q3_psum, 3.0, t3)
             shifted_product(slot(k, 15), q5, 3.0, t5)
             late[k] = (p11, p13, odd_squares)
+            if more:
+                q1, even_squares, a5 = q1_next, even_next, a5_next
             if k < TOKEN_PARTS:
                 regroup_grad_out(k)
             if k > 0 and chunks[k - 1][1] + chunks[k - 1][2] == PASSES:
                 store_group(chunks[k - 1][0])
         finish_chunk(count - 1)
-        quantise_and_multiply(count - 1, nothing)
+        quantise_and_multiply(count - 1)
         store_group(GROUPS - 1)

@@ -207,12 +207,19 @@ def tile_function_kernel(tc, x, w, grad_out, out):
         def with_gpsimd(k):
             return k < count - SCALAR_TAIL
 
+        def twice(k, ap):
+            return ap.unsqueeze(1).to_broadcast([P, 2, size_of(k), SLOT])
+
         def finish_chunk(k):
-            p11, p13, odd_squares = late[k]
+            products, odd_squares = late[k]
             if with_gpsimd(k):
                 evens_on_gpsimd(k, odd_squares, slice(6, 15, 4))
-            minus_x(k, slot(k, 11), p11)
-            minus_x(k, slot(k, 13), p13)
+            nc.vector.tensor_tensor(
+                out=stages[k % STAGES][:, : size_of(k), 11:14:2, :].rearrange("p c q e -> p q c e"),
+                in0=products,
+                in1=twice(k, x_psum[k]),
+                op=ALU.subtract,
+            )
 
         def first_squares(k, between):
             q1 = f32_tile(k, "q1")
@@ -238,9 +245,9 @@ def tile_function_kernel(tc, x, w, grad_out, out):
             q2, q4, q6 = even_squares[:, 0], even_squares[:, 1], even_squares[:, 2]
             t3 = f32_tile(k, "t3")
             shifted_product(t3, q1, 3.0, x_psum[k])
-            t5 = f32_tile(k, "t5")
+            five_seven = f32_tiles(k, "five_seven", 2)
+            t5, t7 = five_seven[:, 0], five_seven[:, 1]
             shifted_product(t5, a5, 1.25, x_psum[k])
-            t7 = f32_tile(k, "t7")
             shifted_product(t7, q2, 2.0, t3)
             odd_squares = f32_tiles(k, "odd_squares", 3)
             q3, q5, q7 = odd_squares[:, 0], odd_squares[:, 1], odd_squares[:, 2]
@@ -286,13 +293,11 @@ def tile_function_kernel(tc, x, w, grad_out, out):
             nc.scalar.copy(out=slot(k, 7), in_=t7)
             if not with_gpsimd(k):
                 round_even(k, 14, q7)
-            p11 = f32_tile(k, "p11")
-            shifted_product(p11, q3_psum, 2.0, t5)
             shifted_product(slot(k, 9), q3_psum, 3.0, t3)
-            p13 = f32_tile(k, "p13")
-            shifted_product(p13, q3_psum, 2.0, t7)
+            products = f32_tiles(k, "products", 2)
+            shifted_product(products, twice(k, q3_psum), 2.0, five_seven)
             shifted_product(slot(k, 15), q5, 3.0, t5)
-            late[k] = (p11, p13, odd_squares)
+            late[k] = (products, odd_squares)
             if more:
                 q1, even_squares, a5 = q1_next, even_next, a5_next
             if k < TOKEN_PARTS:

@@ -50,7 +50,7 @@ def tile_function_kernel(tc, x, w, grad_out, out):
     with ExitStack() as ctx:
         keep = ctx.enter_context(tc.tile_pool(name="keep", bufs=1))
         g_in = ctx.enter_context(tc.tile_pool(name="g_in", bufs=PASSES))
-        g_mid = ctx.enter_context(tc.tile_pool(name="g_mid", bufs=CHUNK_PASSES))
+        g_mid = ctx.enter_context(tc.tile_pool(name="g_mid", bufs=CHUNK_PASSES // 2))
         work = ctx.enter_context(tc.tile_pool(name="work", bufs=2))
         coded = ctx.enter_context(tc.tile_pool(name="coded", bufs=3))
         result = ctx.enter_context(tc.tile_pool(name="result", bufs=4))
@@ -131,8 +131,9 @@ def tile_function_kernel(tc, x, w, grad_out, out):
 
         def regroup_grad_out(part):
             for c in range(part * CHUNK_PASSES, (part + 1) * CHUNK_PASSES):
-                g_grouped[c] = g_mid.tile([P, OUTPUTS, PACK], BF16, name="g_grouped", align_bytes=64)
-                dst = g_grouped[c][:].rearrange("p (a b) j -> p a j b", b=4)
+                if c % 2 == 0:
+                    g_grouped[c] = g_mid.tile([P, 2, OUTPUTS, PACK], BF16, name="g_grouped", align_bytes=64)
+                dst = g_grouped[c - c % 2][:, c % 2].rearrange("p (a b) j -> p a j b", b=4)
                 src = g_raw[c][:].rearrange("p j (a b) -> p a j b", b=4)
                 if c % 2 == 0:
                     nc.scalar.copy(out=dst, in_=src)
@@ -157,35 +158,38 @@ def tile_function_kernel(tc, x, w, grad_out, out):
         def quantise_and_multiply(k):
             group, first, size = chunks[k]
             if group == 0:
-                for c in range(first, first + size):
+                for c in range(first, first + size, 2):
                     nc.vector.quantize_mx(
-                        out=g_codes[:, c, :].bitcast(E5M2_X4),
-                        scales=g_scales[:, c, :],
-                        in_=g_grouped[c][:].rearrange("p o j -> p (o j)"),
+                        out=g_codes[:, c : c + 2, :].rearrange("p c o -> p (c o)").bitcast(E5M2_X4),
+                        scales=g_scales[:, c : c + 2, :].rearrange("p c o -> p (c o)"),
+                        in_=g_grouped[c][:].rearrange("p c o j -> p (c o j)"),
                     )
             b_codes = coded.tile([P, CHUNK_PASSES, N_TILE], U32, name="b_codes", align_bytes=64)
             b_scales = coded.tile([P, CHUNK_PASSES, N_TILE], U8, name="b_scales", align_bytes=64)
             if first == 0:
                 for t in range(O_TILES):
                     sums[group, t] = psum.tile([M_TILE, N_TILE], F32, name="sums%d" % t)
-            for local in range(size):
-                c = first + local
+            together = 2 if (k < count - 2) else 1
+            for head_pass in range(0, size, together):
+                span = slice(head_pass, head_pass + together)
                 nc.vector.quantize_mx(
-                    out=b_codes[:, local, :].bitcast(E4M3_X4),
-                    scales=b_scales[:, local, :],
-                    in_=stages[k % STAGES][:, local, :, :].rearrange("p n e -> p (n e)"),
+                    out=b_codes[:, span, :].rearrange("p c n -> p (c n)").bitcast(E4M3_X4),
+                    scales=b_scales[:, span, :].rearrange("p c n -> p (c n)"),
+                    in_=stages[k % STAGES][:, span, :, :].rearrange("p c n e -> p (c n e)"),
                 )
-                for t in range(O_TILES):
-                    o_cols = slice(t * M_TILE, (t + 1) * M_TILE)
-                    nc.tensor.matmul_mx(
-                        out=sums[group, t][:],
-                        lhsT=g_codes[:, c, o_cols].bitcast(E5M2_X4),
-                        lhsT_scale=g_scales[:, c, o_cols],
-                        rhs=b_codes[:, local, :].bitcast(E4M3_X4),
-                        rhs_scale=b_scales[:, local, :],
-                        start=(c == 0),
-                        stop=(c == PASSES - 1),
-                    )
+                for local in range(head_pass, head_pass + together):
+                    c = first + local
+                    for t in range(O_TILES):
+                        o_cols = slice(t * M_TILE, (t + 1) * M_TILE)
+                        nc.tensor.matmul_mx(
+                            out=sums[group, t][:],
+                            lhsT=g_codes[:, c, o_cols].bitcast(E5M2_X4),
+                            lhsT_scale=g_scales[:, c, o_cols],
+                            rhs=b_codes[:, local, :].bitcast(E4M3_X4),
+                            rhs_scale=b_scales[:, local, :],
+                            start=(c == 0),
+                            stop=(c == PASSES - 1),
+                        )
 
         out_rows = out.rearrange("o i n -> o (i n)")
 

@@ -117,9 +117,12 @@ def tile_function_kernel(tc, x, w, grad_out, out):
         def minus_x(k, dst, a):
             nc.vector.tensor_tensor(out=dst, in0=a, in1=x_psum[k], op=ALU.subtract)
 
-        def evens_on_gpsimd(k, squares, degrees):
+        def fire():
             shot = work.tile([P, 1], F32, name="shot", bufs=4)
             nc.vector.memset(shot[:], 0.5)
+            return shot
+
+        def evens_on_gpsimd(k, squares, degrees, shot):
             nc.gpsimd.tensor_scalar(
                 out=stages[k % STAGES][:, : size_of(k), degrees, :],
                 in0=squares.rearrange("p q c e -> p c q e"),
@@ -155,7 +158,9 @@ def tile_function_kernel(tc, x, w, grad_out, out):
 
         sums = {}
 
-        def quantise_and_multiply(k):
+        second_shot = [None]
+
+        def quantise_and_multiply(k, early_shot):
             group, first, size = chunks[k]
             if group == 0:
                 for c in range(first, first + size, 2):
@@ -172,6 +177,8 @@ def tile_function_kernel(tc, x, w, grad_out, out):
             together = 2 if (k < count - 2) else 1
             for head_pass in range(0, size, together):
                 span = slice(head_pass, head_pass + together)
+                if early_shot and head_pass + together == size:
+                    second_shot[0] = fire()
                 nc.vector.quantize_mx(
                     out=b_codes[:, span, :].rearrange("p c n -> p (c n)").bitcast(E4M3_X4),
                     scales=b_scales[:, span, :].rearrange("p c n -> p (c n)"),
@@ -215,9 +222,9 @@ def tile_function_kernel(tc, x, w, grad_out, out):
             return ap.unsqueeze(1).to_broadcast([P, 2, size_of(k), SLOT])
 
         def finish_chunk(k):
-            products, odd_squares = late[k]
+            products, odd_squares, shot = late[k]
             if with_gpsimd(k):
-                evens_on_gpsimd(k, odd_squares, slice(6, 15, 4))
+                evens_on_gpsimd(k, odd_squares, slice(6, 15, 4), shot if shot is not None else fire())
             nc.vector.tensor_tensor(
                 out=stages[k % STAGES][:, : size_of(k), 11:14:2, :].rearrange("p c q e -> p q c e"),
                 in0=products,
@@ -267,7 +274,7 @@ def tile_function_kernel(tc, x, w, grad_out, out):
             if k == 0:
                 nc.vector.tensor_copy(out=slot(k, 3), in_=t3)
             if k > 0:
-                quantise_and_multiply(k - 1)
+                quantise_and_multiply(k - 1, with_gpsimd(k))
             if k == 0:
                 nc.vector.tensor_copy(out=slot(k, 5), in_=t5)
             square(q5, t5, 2.0, 0.0)
@@ -277,7 +284,7 @@ def tile_function_kernel(tc, x, w, grad_out, out):
             if not (k == 0):
                 nc.scalar.copy(out=slot(k, 5), in_=t5)
             if with_gpsimd(k):
-                evens_on_gpsimd(k, even_squares, slice(4, 13, 4))
+                evens_on_gpsimd(k, even_squares, slice(4, 13, 4), second_shot[0] if k > 0 else fire())
             minus_x(k, t7, t7)
             if not with_gpsimd(k):
                 round_even(k, 4, q2)
@@ -300,8 +307,9 @@ def tile_function_kernel(tc, x, w, grad_out, out):
             shifted_product(slot(k, 9), q3_psum, 3.0, t3)
             products = f32_tiles(k, "products", 2)
             shifted_product(products, twice(k, q3_psum), 2.0, five_seven)
+            shot = fire() if with_gpsimd(k) and k >= TOKEN_PARTS else None
             shifted_product(slot(k, 15), q5, 3.0, t5)
-            late[k] = (products, odd_squares)
+            late[k] = (products, odd_squares, shot)
             if more:
                 q1, even_squares, a5 = q1_next, even_next, a5_next
             if k < TOKEN_PARTS:
@@ -309,5 +317,5 @@ def tile_function_kernel(tc, x, w, grad_out, out):
             if k > 0 and chunks[k - 1][1] + chunks[k - 1][2] == PASSES:
                 store_group(chunks[k - 1][0])
         finish_chunk(count - 1)
-        quantise_and_multiply(count - 1)
+        quantise_and_multiply(count - 1, False)
         store_group(GROUPS - 1)

from contextlib import ExitStack

import concourse.mybir as mybir
from concourse.masks import make_identity

F32 = mybir.dt.float32
BF16 = mybir.dt.bfloat16
U32 = mybir.dt.uint32
U8 = mybir.dt.uint8
E4M3_X4 = mybir.dt.float8_e4m3fn_x4
E5M2_X4 = mybir.dt.float8_e5m2_x4
ACT = mybir.ActivationFunctionType
ALU = mybir.AluOpType

TOKENS, FEATURES, OUTPUTS, DEGREES = 4096, 128, 512, 16
P = 128
PACK = 4
K_PASS = P * PACK
PASSES = TOKENS // K_PASS
N_TILE = 512
M_TILE = 128
O_TILES = OUTPUTS // M_TILE
GROUP = N_TILE // DEGREES
GROUPS = FEATURES // GROUP
SLOT = GROUP * PACK
TOKEN_PARTS = 2
CHUNK_PASSES = PASSES // TOKEN_PARTS
CHUNKS = GROUPS * TOKEN_PARTS
STAGES = 3

FLOPS = 2 * TOKENS * OUTPUTS * FEATURES * DEGREES
BYTES = 2 * TOKENS * FEATURES + 2 * TOKENS * OUTPUTS + 4 * OUTPUTS * FEATURES * DEGREES


X_BANKS = 3
SIZES = (4, 4)
LAST_SIZES = (4, 2, 2)
SCALAR_TAIL = 1


def tile_function_kernel(tc, x, w, grad_out, out):
    nc = tc.nc
    chunks = []
    for group in range(GROUPS):
        first = 0
        for size in LAST_SIZES if group == GROUPS - 1 else SIZES:
            chunks.append((group, first, size))
            first += size
    count = len(chunks)
    with ExitStack() as ctx:
        keep = ctx.enter_context(tc.tile_pool(name="keep", bufs=1))
        g_in = ctx.enter_context(tc.tile_pool(name="g_in", bufs=PASSES))
        g_mid = ctx.enter_context(tc.tile_pool(name="g_mid", bufs=CHUNK_PASSES // 2))
        work = ctx.enter_context(tc.tile_pool(name="work", bufs=2))
        coded = ctx.enter_context(tc.tile_pool(name="coded", bufs=3))
        result = ctx.enter_context(tc.tile_pool(name="result", bufs=4))
        psum = ctx.enter_context(tc.psum_pool(name="psum", bufs=1))
        ctx.enter_context(tc.manual_schedule())

        x_rows = x.rearrange("(c p j) i -> p c j i", p=P, j=PACK)
        x_raw = keep.tile([P, PASSES, PACK, FEATURES], BF16, name="x_raw")
        g_rows = grad_out.rearrange("(c p j) o -> c p j o", p=P, j=PACK)
        g_raw = []
        for part in range(TOKEN_PARTS):
            passes = slice(part * CHUNK_PASSES, (part + 1) * CHUNK_PASSES)
            nc.sync.dma_start(out=x_raw[:, passes], in_=x_rows[:, passes])
        for c in range(PASSES):
            g_raw.append(g_in.tile([P, PACK, OUTPUTS], BF16, name="g_raw"))
            nc.sync.dma_start(out=g_raw[c][:], in_=g_rows[c])

        ident = keep.tile([P, P], BF16, name="ident")
        make_identity(nc, ident[:])
        ident32 = keep.tile([P, P], F32, name="ident32")
        make_identity(nc, ident32[:])
        minus = {}
        for value in (1.0, 2.0, 2.5):
            minus[value] = keep.tile([P, 1], F32, name="minus_%d" % int(10 * value))
            nc.vector.memset(minus[value][:], -value)
        stages = []
        for s in range(STAGES):
            stages.append(
                keep.tile([P, CHUNK_PASSES, DEGREES, SLOT], BF16, name="stage%d" % s, align_bytes=64)
            )
            nc.vector.memset(stages[s][:, :, 0, :], 1.0)

        g_codes = keep.tile([P, PASSES, OUTPUTS], U32, name="g_codes", align_bytes=64)
        g_scales = keep.tile([P, PASSES, OUTPUTS], U8, name="g_scales", align_bytes=64)
        g_grouped = {}
        x_psum = {}

        def size_of(k):
            return chunks[k][2]

        def slot(k, n):
            return stages[k % STAGES][:, : size_of(k), n, :]

        def f32_tile(k, name):
            whole = work.tile([P, CHUNK_PASSES, SLOT], F32, name=name)
            return whole[:, : size_of(k), :]

        def f32_tiles(k, name, how_many):
            whole = work.tile([P, how_many, CHUNK_PASSES, SLOT], F32, name=name)
            return whole[:, :, : size_of(k), :]

        def square(dst, src, scale, shift):
            if shift == 0.0:
                nc.scalar.activation(out=dst, in_=src, func=ACT.Square, scale=scale)
            else:
                nc.scalar.activation(out=dst, in_=src, func=ACT.Square, scale=scale, bias=minus[shift][:])

        def round_even(k, n, q_half):
            nc.scalar.activation(out=slot(k, n), in_=q_half, func=ACT.Identity, scale=0.5, bias=minus[1.0][:])

        def shifted_product(dst, a, shift, b):
            nc.vector.scalar_tensor_tensor(out=dst, in0=a, scalar=shift, in1=b, op0=ALU.subtract, op1=ALU.mult)

        def minus_x(k, dst, a):
            nc.vector.tensor_tensor(out=dst, in0=a, in1=x_psum[k], op=ALU.subtract)

        def fire():
            shot = work.tile([P, 1], F32, name="shot", bufs=4)
            nc.vector.memset(shot[:], 0.5)
            return shot

        def evens_on_gpsimd(k, squares, degrees, shot):
            nc.gpsimd.tensor_scalar(
                out=stages[k % STAGES][:, : size_of(k), degrees, :],
                in0=squares.rearrange("p q c e -> p c q e"),
                scalar1=shot[:, 0:1],
                scalar2=-1.0,
                op0=ALU.mult,
                op1=ALU.add,
            )

        def regroup_grad_out(part):
            for c in range(part * CHUNK_PASSES, (part + 1) * CHUNK_PASSES):
                if c % 2 == 0:
                    g_grouped[c] = g_mid.tile([P, 2, OUTPUTS, PACK], BF16, name="g_grouped", align_bytes=64)
                dst = g_grouped[c - c % 2][:, c % 2].rearrange("p (a b) j -> p a j b", b=4)
                src = g_raw[c][:].rearrange("p j (a b) -> p a j b", b=4)
                if c % 2 == 0:
                    nc.scalar.copy(out=dst, in_=src)
                else:
                    nc.vector.tensor_copy(out=dst, in_=src)

        def degree_one(k):
            group, first, size = chunks[k]
            features = slice(group * GROUP, (group + 1) * GROUP)
            dst = slot(k, 1).rearrange("p c (i j) -> p c i j", j=PACK)
            src = x_raw[:, first : first + size, :, features].rearrange("p c j i -> p c i j")
            if k > 1:
                nc.scalar.copy(out=dst, in_=src)
            else:
                nc.vector.tensor_copy(out=dst, in_=src)
            bank = psum.tile([P, CHUNK_PASSES, SLOT], F32, name="xp", bufs=X_BANKS)
            x_psum[k] = bank[:, :size, :]
            nc.tensor.matmul(out=x_psum[k], lhsT=ident[:], rhs=slot(k, 1), start=True, stop=True)

        sums = {}

        second_shot = [None]

        def quantise_and_multiply(k, early_shot):
            group, first, size = chunks[k]
            if group == 0:
                for c in range(first, first + size, 2):
                    nc.vector.quantize_mx(
                        out=g_codes[:, c : c + 2, :].rearrange("p c o -> p (c o)").bitcast(E5M2_X4),
                        scales=g_scales[:, c : c + 2, :].rearrange("p c o -> p (c o)"),
                        in_=g_grouped[c][:].rearrange("p c o j -> p (c o j)"),
                    )
            b_codes = coded.tile([P, CHUNK_PASSES, N_TILE], U32, name="b_codes", align_bytes=64)
            b_scales = coded.tile([P, CHUNK_PASSES, N_TILE], U8, name="b_scales", align_bytes=64)
            if first == 0:
                for t in range(O_TILES):
                    sums[group, t] = psum.tile([M_TILE, N_TILE], F32, name="sums%d" % t)
            together = 2 if (k < count - 2) else 1
            for head_pass in range(0, size, together):
                span = slice(head_pass, head_pass + together)
                if early_shot and head_pass + together == size:
                    second_shot[0] = fire()
                nc.vector.quantize_mx(
                    out=b_codes[:, span, :].rearrange("p c n -> p (c n)").bitcast(E4M3_X4),
                    scales=b_scales[:, span, :].rearrange("p c n -> p (c n)"),
                    in_=stages[k % STAGES][:, span, :, :].rearrange("p c n e -> p (c n e)"),
                )
                for local in range(head_pass, head_pass + together):
                    c = first + local
                    for t in range(O_TILES):
                        o_cols = slice(t * M_TILE, (t + 1) * M_TILE)
                        nc.tensor.matmul_mx(
                            out=sums[group, t][:],
                            lhsT=g_codes[:, c, o_cols].bitcast(E5M2_X4),
                            lhsT_scale=g_scales[:, c, o_cols],
                            rhs=b_codes[:, local, :].bitcast(E4M3_X4),
                            rhs_scale=b_scales[:, local, :],
                            start=(c == 0),
                            stop=(c == PASSES - 1),
                        )

        out_rows = out.rearrange("o i n -> o (i n)")

        def store_group(group):
            for t in range(O_TILES):
                ordered = result.tile([M_TILE, GROUP, DEGREES], F32, name="ordered")
                by_feature = sums[group, t][:].rearrange("p (n i) -> p i n", n=DEGREES)
                if group == GROUPS - 1 and t % 2 == 1:
                    nc.vector.tensor_copy(out=ordered[:], in_=by_feature)
                else:
                    nc.scalar.copy(out=ordered[:], in_=by_feature)
                nc.sync.dma_start(
                    out=out_rows[t * M_TILE : (t + 1) * M_TILE, group * N_TILE : (group + 1) * N_TILE],
                    in_=ordered[:].rearrange("p i n -> p (i n)"),
                )

        late = {}

        def with_gpsimd(k):
            return k < count - SCALAR_TAIL

        def twice(k, ap):
            return ap.unsqueeze(1).to_broadcast([P, 2, size_of(k), SLOT])

        def finish_chunk(k):
            products, odd_squares, shot = late[k]
            if with_gpsimd(k):
                evens_on_gpsimd(k, odd_squares, slice(6, 15, 4), shot if shot is not None else fire())
            nc.vector.tensor_tensor(
                out=stages[k % STAGES][:, : size_of(k), 11:14:2, :].rearrange("p c q e -> p q c e"),
                in0=products,
                in1=twice(k, x_psum[k]),
                op=ALU.subtract,
            )

        def first_squares(k, between):
            q1 = f32_tile(k, "q1")
            square(q1, slot(k, 1), 2.0, 0.0)
            between()
            even_squares = f32_tiles(k, "even_squares", 3)
            square(even_squares[:, 0], q1, 1.0, 2.0)
            a5 = f32_tile(k, "a5")
            square(a5, q1, 1.0, 2.5)
            return q1, even_squares, a5

        def nothing():
            return None

        degree_one(0)
        q1, even_squares, a5 = first_squares(0, nothing)
        for k in range(count):
            more = k + 1 < count
            if more:
                degree_one(k + 1)
            if k > 0:
                finish_chunk(k - 1)
            q2, q4, q6 = even_squares[:, 0], even_squares[:, 1], even_squares[:, 2]
            t3 = f32_tile(k, "t3")
            shifted_product(t3, q1, 3.0, x_psum[k])
            five_seven = f32_tiles(k, "five_seven", 2)
            t5, t7 = five_seven[:, 0], five_seven[:, 1]
            shifted_product(t5, a5, 1.25, x_psum[k])
            shifted_product(t7, q2, 2.0, t3)
            odd_squares = f32_tiles(k, "odd_squares", 3)
            q3, q5, q7 = odd_squares[:, 0], odd_squares[:, 1], odd_squares[:, 2]
            square(q3, t3, 2.0, 0.0)
            square(q4, q2, 1.0, 2.0)
            square(q6, q3, 1.0, 2.0)
            if with_gpsimd(k):
                bank = psum.tile([P, CHUNK_PASSES, SLOT], F32, name="q3p")
                q3_psum = bank[:, : size_of(k), :]
                nc.tensor.matmul(out=q3_psum, lhsT=ident32[:], rhs=q3, start=True, stop=True)
            else:
                q3_psum = q3
            if k == 0:
                nc.vector.tensor_copy(out=slot(k, 3), in_=t3)
            if k > 0:
                quantise_and_multiply(k - 1, with_gpsimd(k))
            if k == 0:
                nc.vector.tensor_copy(out=slot(k, 5), in_=t5)
            square(q5, t5, 2.0, 0.0)
            if not (k == 0):
                nc.scalar.copy(out=slot(k, 3), in_=t3)
            round_even(k, 2, q1)
            if not (k == 0):
                nc.scalar.copy(out=slot(k, 5), in_=t5)
            if with_gpsimd(k):
                evens_on_gpsimd(k, even_squares, slice(4, 13, 4), second_shot[0] if k > 0 else fire())
            minus_x(k, t7, t7)
            if not with_gpsimd(k):
                round_even(k, 4, q2)
                round_even(k, 8, q4)
                round_even(k, 6, q3)
                round_even(k, 10, q5)
                round_even(k, 12, q6)
            old = (q3, q5, q7, t7, k)

            def seventh(old=old):
                square(old[2], old[3], 2.0, 0.0)

            if more:
                q1_next, even_next, a5_next = first_squares(k + 1, seventh)
            else:
                seventh()
            nc.scalar.copy(out=slot(k, 7), in_=t7)
            if not with_gpsimd(k):
                round_even(k, 14, q7)
            shifted_product(slot(k, 9), q3_psum, 3.0, t3)
            products = f32_tiles(k, "products", 2)
            shifted_product(products, twice(k, q3_psum), 2.0, five_seven)
            shot = fire() if with_gpsimd(k) and k >= TOKEN_PARTS else None
            shifted_product(slot(k, 15), q5, 3.0, t5)
            late[k] = (products, odd_squares, shot)
            if more:
                q1, even_squares, a5 = q1_next, even_next, a5_next
            if k < TOKEN_PARTS:
                regroup_grad_out(k)
            if k > 0 and chunks[k - 1][1] + chunks[k - 1][2] == PASSES:
                store_group(chunks[k - 1][0])
        finish_chunk(count - 1)
        quantise_and_multiply(count - 1, False)
        store_group(GROUPS - 1)
